import numpy as np
import ml_dtypes


def mxq(x, axis, fmt="e4m3"):
    dtype, down = {"e4m3": (ml_dtypes.float8_e4m3fn, 7), "e5m2": (ml_dtypes.float8_e5m2, 14)}[fmt]
    v = np.moveaxis(np.asarray(x, np.float32).astype(ml_dtypes.bfloat16).astype(np.float64), axis, -1)
    blocks = v.reshape(v.shape[:-1] + (-1, 32))
    amax = np.abs(blocks).max(-1, keepdims=True)
    byte = np.maximum(np.where(amax > 0, np.frexp(amax)[1] - 1 + 127, 0) - down, 1)
    scale = np.exp2(byte - 127.0)
    codes = (blocks / scale).astype(np.float32).astype(dtype).astype(np.float64)
    return np.moveaxis((codes * scale).reshape(v.shape), -1, axis)


WIDE = False


def mx_kscale(k):
    if not WIDE:
        return np.ones(k)
    levels = np.array([20, -20, 10, -10, 0])
    a = np.random.permutation(np.resize(levels, k // 512 * 4)).reshape(k // 512, 4)
    idx = np.arange(k)
    return np.exp2(a[idx // 512, idx % 128 // 32])


BF16 = ml_dtypes.bfloat16


def bf(x):
    return np.asarray(x, np.float32).astype(BF16)


def f64(x):
    return np.asarray(x).astype(np.float64)


B, F, H, C = 1024, 1024, 512, 10
EPS = 4.0 / 30.0
P_KEEP = 0.95


def client1(x1, W1, b1, noise_std, rr_uniform):
    a = f64(x1) @ f64(W1) + f64(b1)
    n = np.sum(np.abs(a), axis=1)
    sens = np.max(n) - np.min(n)
    keep = np.where(f64(rr_uniform) < P_KEEP, 1.0, 0.0)
    return (a + f64(noise_std) * (sens / EPS)) * keep


def client2(x2, W2, b2):
    return f64(x2) @ f64(W2) + f64(b2)


def setup_inputs():
    s = mx_kscale(B)[:, None]
    ns = EPS / (6.0 * np.sqrt(H))
    x1 = bf(np.random.standard_normal((B, F)))
    x2_0 = bf(np.random.standard_normal((B, F)))
    W1 = bf(np.random.standard_normal((F, H)) / np.sqrt(F))
    b1 = bf(np.random.standard_normal(H) * 0.3)
    W2 = bf(np.random.standard_normal((F, H)) / np.sqrt(F))
    b2 = bf(np.random.standard_normal(H) * 0.3)
    noise_std = bf(np.random.laplace(size=(B, H)) * ns)
    rr_uniform = bf(np.random.uniform(size=H))
    g = bf(np.random.standard_normal((B, H)) * np.exp2(np.random.randint(-12, 1, (B, 1))) / s)
    c = client1(x1, W1, b1, noise_std, rr_uniform)
    d = client2(x2_0, W2, b2)
    return {"x1": x1, "x2": bf(f64(x2_0) * s), "W1": W1, "b1": b1, "W2": W2, "b2": b2,
            "noise_std": noise_std, "rr_uniform": rr_uniform,
            "c": np.asarray(c, np.float32), "d": np.asarray(d, np.float32), "grad_out": g}


def reference(x1, x2, W1, b1, W2, b2, noise_std, rr_uniform, c, d, grad_out):
    cf, df = f64(c), f64(d)
    m = np.where(df < cf, 1.0, 0.0) + np.where(df == cf, 0.5, 0.0)
    dz = f64(grad_out) * m
    return mxq(f64(x2), 0, "e4m3").T @ mxq(dz, 0, "e5m2")

@@ -1,0 +1,157 @@
+from contextlib import ExitStack
+
+import concourse.mybir as mybir
+
+F32 = mybir.dt.float32
+BF16 = mybir.dt.bfloat16
+U32 = mybir.dt.uint32
+U8 = mybir.dt.uint8
+E4M3_X4 = mybir.dt.float8_e4m3fn_x4
+E5M2_X4 = mybir.dt.float8_e5m2_x4
+ALU = mybir.AluOpType
+ACT = mybir.ActivationFunctionType
+
+B, F, H = 1024, 1024, 512
+P = 128
+PACK = 4
+K_PASS = P * PACK
+PASSES = B // K_PASS
+ROW_PAIRS = 2
+HALVES = 2
+HALF = H // HALVES
+UNIT = 256
+UNITS = F // UNIT
+M_TILE = 128
+M_TILES = F // M_TILE
+
+FLOPS = 2 * B * F * H
+BYTES = 2 * B * F + 2 * 4 * B * H + 2 * B * H + 4 * F * H
+
+
+def tile_splitnn_pa_v_kernel(
+    tc, x1, x2, W1, b1, W2, b2, noise_std, rr_uniform, c, d, grad_out, out
+):
+    nc = tc.nc
+
+    def pass_rows(dram, k_pass):
+        rows = dram[k_pass * K_PASS : (k_pass + 1) * K_PASS, :]
+        return rows.rearrange("(p j) w -> p j w", j=PACK)
+
+    with ExitStack() as ctx:
+        keep = ctx.enter_context(tc.tile_pool(name="keep", bufs=1))
+        psum = ctx.enter_context(tc.psum_pool(name="psum", bufs=1))
+        ctx.enter_context(tc.manual_schedule())
+
+        c_raw = [keep.tile([P, PACK, H], F32, name="c_raw%d" % k) for k in range(PASSES)]
+        d_raw = [keep.tile([P, PACK, H], F32, name="d_raw%d" % k) for k in range(PASSES)]
+        g_raw = [keep.tile([P, PACK, H], BF16, name="g_raw%d" % k) for k in range(PASSES)]
+        x_raw = [keep.tile([P, PACK, F], BF16, name="x_raw%d" % k) for k in range(PASSES)]
+        diff = [
+            [keep.tile([P, PACK, HALF], F32, name="diff%d%d" % (k, h)) for h in range(HALVES)]
+            for k in range(PASSES)
+        ]
+        sign = [
+            [keep.tile([P, PACK, HALF], BF16, name="sign%d%d" % (k, h)) for h in range(HALVES)]
+            for k in range(PASSES)
+        ]
+        dz_grouped = [
+            keep.tile([P, H, PACK], BF16, name="dz_grouped%d" % k, align_bytes=64)
+            for k in range(PASSES)
+        ]
+        x_grouped = [
+            keep.tile([P, F, PACK], BF16, name="x_grouped%d" % k, align_bytes=64)
+            for k in range(PASSES)
+        ]
+        dz_codes = keep.tile([P, PASSES, H], U32, name="dz_codes", align_bytes=64)
+        dz_scales = keep.tile([P, PASSES, H], U8, name="dz_scales", align_bytes=64)
+        x_codes = keep.tile([P, PASSES, F], U32, name="x_codes", align_bytes=64)
+        x_scales = keep.tile([P, PASSES, F], U8, name="x_scales", align_bytes=64)
+        acc = [psum.tile([M_TILE, H], F32, name="acc%d" % m) for m in range(M_TILES)]
+        result = [keep.tile([M_TILE, H], F32, name="result%d" % m) for m in range(M_TILES)]
+
+        for k in range(PASSES):
+            for a in range(ROW_PAIRS):
+                pair = slice(2 * a, 2 * a + 2)
+                nc.sync.dma_start(out=c_raw[k][:, pair, :], in_=pass_rows(c, k)[:, pair, :])
+                nc.sync.dma_start(out=d_raw[k][:, pair, :], in_=pass_rows(d, k)[:, pair, :])
+            nc.sync.dma_start(out=g_raw[k][:], in_=pass_rows(grad_out, k))
+        for u in range(UNITS):
+            cols = slice(u * UNIT, (u + 1) * UNIT)
+            for k in range(PASSES):
+                nc.sync.dma_start(out=x_raw[k][:, :, cols], in_=pass_rows(x2, k)[:, :, cols])
+
+        def compare(k, a, h):
+            pair = slice(2 * a, 2 * a + 2)
+            cols = slice(h * HALF, (h + 1) * HALF)
+            nc.vector.tensor_tensor(
+                out=diff[k][h][:, pair, :], in0=c_raw[k][:, pair, cols], in1=d_raw[k][:, pair, cols],
+                op=ALU.subtract,
+            )
+            nc.scalar.activation(out=sign[k][h][:, pair, :], in_=diff[k][h][:, pair, :], func=ACT.Sign)
+
+        def masked_gradient(k, h):
+            cols = slice(h * HALF, (h + 1) * HALF)
+            nc.vector.scalar_tensor_tensor(
+                out=dz_grouped[k][:, cols, :],
+                in0=sign[k][h][:].rearrange("p j w -> p w j"),
+                scalar=1.0,
+                in1=g_raw[k][:, :, cols].rearrange("p j w -> p w j"),
+                op0=ALU.add,
+                op1=ALU.mult,
+            )
+
+        def quantise_dz(k):
+            nc.vector.quantize_mx(
+                out=dz_codes[:, k, :].bitcast(E5M2_X4),
+                scales=dz_scales[:, k, :],
+                in_=dz_grouped[k][:].rearrange("p w j -> p (w j)"),
+            )
+
+        def regroup_x(copy, k, u):
+            cols = slice(u * UNIT, (u + 1) * UNIT)
+            copy(
+                out=x_grouped[k][:, cols, :].rearrange("p (q i) j -> p q j i", i=4),
+                in_=x_raw[k][:, :, cols].rearrange("p j (q i) -> p q j i", i=4),
+            )
+
+        def quantise_x(k, u):
+            cols = slice(u * UNIT, (u + 1) * UNIT)
+            nc.vector.quantize_mx(
+                out=x_codes[:, k, cols].bitcast(E4M3_X4),
+                scales=x_scales[:, k, cols],
+                in_=x_grouped[k][:, cols, :].rearrange("p w j -> p (w j)"),
+            )
+
+        def multiply(k, m):
+            rows = slice(m * M_TILE, (m + 1) * M_TILE)
+            nc.tensor.matmul_mx(
+                out=acc[m][:],
+                lhsT=x_codes[:, k, rows].bitcast(E4M3_X4),
+                lhsT_scale=x_scales[:, k, rows],
+                rhs=dz_codes[:, k, :].bitcast(E5M2_X4),
+                rhs_scale=dz_scales[:, k, :],
+                start=(k == 0),
+                stop=(k == PASSES - 1),
+            )
+
+        for k in range(PASSES):
+            for a in range(ROW_PAIRS):
+                for h in range(HALVES):
+                    compare(k, a, h)
+            for h in range(HALVES):
+                masked_gradient(k, h)
+            quantise_dz(k)
+
+        for u in range(UNITS):
+            for k in range(PASSES):
+                regroup_x(nc.scalar.copy if u == 0 else nc.vector.tensor_copy, k, u)
+            for k in range(PASSES):
+                quantise_x(k, u)
+            for m in range(u * UNIT // M_TILE, (u + 1) * UNIT // M_TILE):
+                for k in range(PASSES):
+                    multiply(k, m)
+                if m < M_TILES - 1:
+                    nc.scalar.mul(out=result[m][:], in_=acc[m][:], mul=0.5)
+                else:
+                    nc.vector.tensor_scalar_mul(out=result[m][:], in0=acc[m][:], scalar1=0.5)
+                nc.sync.dma_start(out=out[m * M_TILE : (m + 1) * M_TILE, :], in_=result[m][:])

@@ -23,6 +23,7 @@ UNIT = 256
 UNITS = F // UNIT
 M_TILE = 128
 M_TILES = F // M_TILE
+SCALAR_PIECES = 3
 
 FLOPS = 2 * B * F * H
 BYTES = 2 * B * F + 2 * 4 * B * H + 2 * B * H + 4 * F * H
@@ -142,9 +143,14 @@ def tile_splitnn_pa_v_kernel(
                 masked_gradient(k, h)
             quantise_dz(k)
 
+        pieces = [(k, u) for u in range(UNITS) for k in range(PASSES)]
+        for k, u in pieces[:SCALAR_PIECES]:
+            regroup_x(nc.scalar.copy, k, u)
+
         for u in range(UNITS):
             for k in range(PASSES):
-                regroup_x(nc.scalar.copy if u == 0 else nc.vector.tensor_copy, k, u)
+                if (k, u) in pieces[SCALAR_PIECES:]:
+                    regroup_x(nc.vector.tensor_copy, k, u)
             for k in range(PASSES):
                 quantise_x(k, u)
             for m in range(u * UNIT // M_TILE, (u + 1) * UNIT // M_TILE):

@@ -23,7 +23,7 @@ UNIT = 256
 UNITS = F // UNIT
 M_TILE = 128
 M_TILES = F // M_TILE
-SCALAR_PIECES = 3
+SCALAR_PIECES = 4
 
 FLOPS = 2 * B * F * H
 BYTES = 2 * B * F + 2 * 4 * B * H + 2 * B * H + 4 * F * H
@@ -41,7 +41,6 @@ def tile_splitnn_pa_v_kernel(
     with ExitStack() as ctx:
         keep = ctx.enter_context(tc.tile_pool(name="keep", bufs=1))
         psum = ctx.enter_context(tc.psum_pool(name="psum", bufs=1))
-        ctx.enter_context(tc.manual_schedule())
 
         c_raw = [keep.tile([P, PACK, H], F32, name="c_raw%d" % k) for k in range(PASSES)]
         d_raw = [keep.tile([P, PACK, H], F32, name="d_raw%d" % k) for k in range(PASSES)]

@@ -23,7 +23,7 @@ UNIT = 256
 UNITS = F // UNIT
 M_TILE = 128
 M_TILES = F // M_TILE
-SCALAR_PIECES = 4
+SCALAR_PIECES = 5
 
 FLOPS = 2 * B * F * H
 BYTES = 2 * B * F + 2 * 4 * B * H + 2 * B * H + 4 * F * H
@@ -69,16 +69,19 @@ def tile_splitnn_pa_v_kernel(
         acc = [psum.tile([M_TILE, H], F32, name="acc%d" % m) for m in range(M_TILES)]
         result = [keep.tile([M_TILE, H], F32, name="result%d" % m) for m in range(M_TILES)]
 
+        pieces = [(0, 0), (0, 1), (1, 0), (1, 1)] + [(k, u) for u in range(2, UNITS) for k in range(PASSES)]
+
         for k in range(PASSES):
             for a in range(ROW_PAIRS):
                 pair = slice(2 * a, 2 * a + 2)
                 nc.sync.dma_start(out=c_raw[k][:, pair, :], in_=pass_rows(c, k)[:, pair, :])
                 nc.sync.dma_start(out=d_raw[k][:, pair, :], in_=pass_rows(d, k)[:, pair, :])
             nc.sync.dma_start(out=g_raw[k][:], in_=pass_rows(grad_out, k))
-        for u in range(UNITS):
+            if k == 0:
+                nc.sync.dma_start(out=x_raw[0][:, :, 0 : 2 * UNIT], in_=pass_rows(x2, 0)[:, :, 0 : 2 * UNIT])
+        for k, u in pieces[2:]:
             cols = slice(u * UNIT, (u + 1) * UNIT)
-            for k in range(PASSES):
-                nc.sync.dma_start(out=x_raw[k][:, :, cols], in_=pass_rows(x2, k)[:, :, cols])
+            nc.sync.dma_start(out=x_raw[k][:, :, cols], in_=pass_rows(x2, k)[:, :, cols])
 
         def compare(k, a, h):
             pair = slice(2 * a, 2 * a + 2)
@@ -134,15 +137,26 @@ def tile_splitnn_pa_v_kernel(
                 stop=(k == PASSES - 1),
             )
 
+        def warm_up(moving):
+            nc.tensor.matmul(
+                out=acc[M_TILES - 1][:], lhsT=g_raw[0][:, 0, 0:M_TILE], rhs=moving, start=True, stop=True
+            )
+
         for k in range(PASSES):
             for a in range(ROW_PAIRS):
                 for h in range(HALVES):
                     compare(k, a, h)
+            if k == PASSES - 1:
+                for h in range(HALVES):
+                    warm_up(sign[k][h][:, 2:4, :].rearrange("p j w -> p (j w)"))
             for h in range(HALVES):
                 masked_gradient(k, h)
+                if k == PASSES - 1:
+                    for part in range(2):
+                        cols = slice(h * HALF + part * (HALF // 2), h * HALF + (part + 1) * (HALF // 2))
+                        warm_up(dz_grouped[k][:, cols, :].rearrange("p w j -> p (w j)"))
             quantise_dz(k)
 
-        pieces = [(k, u) for u in range(UNITS) for k in range(PASSES)]
         for k, u in pieces[:SCALAR_PIECES]:
             regroup_x(nc.scalar.copy, k, u)
 

@@ -103,11 +103,12 @@ def tile_splitnn_pa_v_kernel(
                 op1=ALU.mult,
             )
 
-        def quantise_dz(k):
+        def quantise_dz(k, h):
+            cols = slice(h * HALF, (h + 1) * HALF)
             nc.vector.quantize_mx(
-                out=dz_codes[:, k, :].bitcast(E5M2_X4),
-                scales=dz_scales[:, k, :],
-                in_=dz_grouped[k][:].rearrange("p w j -> p (w j)"),
+                out=dz_codes[:, k, cols].bitcast(E5M2_X4),
+                scales=dz_scales[:, k, cols],
+                in_=dz_grouped[k][:, cols, :].rearrange("p w j -> p (w j)"),
             )
 
         def regroup_x(copy, k, u):
@@ -155,7 +156,8 @@ def tile_splitnn_pa_v_kernel(
                     for part in range(2):
                         cols = slice(h * HALF + part * (HALF // 2), h * HALF + (part + 1) * (HALF // 2))
                         warm_up(dz_grouped[k][:, cols, :].rearrange("p w j -> p (w j)"))
-            quantise_dz(k)
+            for h in range(HALVES):
+                quantise_dz(k, h)
 
         for k, u in pieces[:SCALAR_PIECES]:
             regroup_x(nc.scalar.copy, k, u)

@@ -25,6 +25,8 @@ M_TILE = 128
 M_TILES = F // M_TILE
 SCALAR_PIECES = 5
 
+STEEP = 2.0**100
+
 FLOPS = 2 * B * F * H
 BYTES = 2 * B * F + 2 * 4 * B * H + 2 * B * H + 4 * F * H
 
@@ -50,8 +52,8 @@ def tile_splitnn_pa_v_kernel(
             [keep.tile([P, PACK, HALF], F32, name="diff%d%d" % (k, h)) for h in range(HALVES)]
             for k in range(PASSES)
         ]
-        sign = [
-            [keep.tile([P, PACK, HALF], BF16, name="sign%d%d" % (k, h)) for h in range(HALVES)]
+        share = [
+            [keep.tile([P, PACK, HALF], BF16, name="share%d%d" % (k, h)) for h in range(HALVES)]
             for k in range(PASSES)
         ]
         dz_grouped = [
@@ -90,17 +92,15 @@ def tile_splitnn_pa_v_kernel(
                 out=diff[k][h][:, pair, :], in0=c_raw[k][:, pair, cols], in1=d_raw[k][:, pair, cols],
                 op=ALU.subtract,
             )
-            nc.scalar.activation(out=sign[k][h][:, pair, :], in_=diff[k][h][:, pair, :], func=ACT.Sign)
+            nc.scalar.activation(out=share[k][h][:, pair, :], in_=diff[k][h][:, pair, :], func=ACT.Sigmoid, scale=STEEP)
 
         def masked_gradient(k, h):
             cols = slice(h * HALF, (h + 1) * HALF)
-            nc.vector.scalar_tensor_tensor(
-                out=dz_grouped[k][:, cols, :],
-                in0=sign[k][h][:].rearrange("p j w -> p w j"),
-                scalar=1.0,
-                in1=g_raw[k][:, :, cols].rearrange("p j w -> p w j"),
-                op0=ALU.add,
-                op1=ALU.mult,
+            nc.vector.tensor_tensor(
+                out=dz_grouped[k][:, cols, :].rearrange("p (q i) j -> p q j i", i=4),
+                in0=share[k][h][:].rearrange("p j (q i) -> p q j i", i=4),
+                in1=g_raw[k][:, :, cols].rearrange("p j (q i) -> p q j i", i=4),
+                op=ALU.mult,
             )
 
         def quantise_dz(k, h):
@@ -149,7 +149,7 @@ def tile_splitnn_pa_v_kernel(
                     compare(k, a, h)
             if k == PASSES - 1:
                 for h in range(HALVES):
-                    warm_up(sign[k][h][:, 2:4, :].rearrange("p j w -> p (j w)"))
+                    warm_up(share[k][h][:, 2:4, :].rearrange("p j w -> p (j w)"))
             for h in range(HALVES):
                 masked_gradient(k, h)
                 if k == PASSES - 1:
@@ -172,7 +172,7 @@ def tile_splitnn_pa_v_kernel(
                 for k in range(PASSES):
                     multiply(k, m)
                 if m < M_TILES - 1:
-                    nc.scalar.mul(out=result[m][:], in_=acc[m][:], mul=0.5)
+                    nc.scalar.copy(out=result[m][:], in_=acc[m][:])
                 else:
-                    nc.vector.tensor_scalar_mul(out=result[m][:], in0=acc[m][:], scalar1=0.5)
+                    nc.vector.tensor_copy(out=result[m][:], in_=acc[m][:])
                 nc.sync.dma_start(out=out[m * M_TILE : (m + 1) * M_TILE, :], in_=result[m][:])

@@ -1,6 +1,7 @@
 from contextlib import ExitStack
 
 import concourse.mybir as mybir
+from concourse.masks import make_identity
 
 F32 = mybir.dt.float32
 BF16 = mybir.dt.bfloat16
@@ -16,15 +17,12 @@ P = 128
 PACK = 4
 K_PASS = P * PACK
 PASSES = B // K_PASS
-ROW_PAIRS = 2
 HALVES = 2
 HALF = H // HALVES
 UNIT = 256
 UNITS = F // UNIT
 M_TILE = 128
 M_TILES = F // M_TILE
-SCALAR_PIECES = 5
-
 STEEP = 2.0**100
 
 FLOPS = 2 * B * F * H
@@ -40,6 +38,14 @@ def tile_splitnn_pa_v_kernel(
         rows = dram[k_pass * K_PASS : (k_pass + 1) * K_PASS, :]
         return rows.rearrange("(p j) w -> p j w", j=PACK)
 
+    def half(h):
+        return slice(h * HALF, (h + 1) * HALF)
+
+    def unit(u):
+        return slice(u * UNIT, (u + 1) * UNIT)
+
+    low, high = slice(0, 2), slice(2, 4)
+
     with ExitStack() as ctx:
         keep = ctx.enter_context(tc.tile_pool(name="keep", bufs=1))
         psum = ctx.enter_context(tc.psum_pool(name="psum", bufs=1))
@@ -47,87 +53,102 @@ def tile_splitnn_pa_v_kernel(
         c_raw = [keep.tile([P, PACK, H], F32, name="c_raw%d" % k) for k in range(PASSES)]
         d_raw = [keep.tile([P, PACK, H], F32, name="d_raw%d" % k) for k in range(PASSES)]
         g_raw = [keep.tile([P, PACK, H], BF16, name="g_raw%d" % k) for k in range(PASSES)]
-        x_raw = [keep.tile([P, PACK, F], BF16, name="x_raw%d" % k) for k in range(PASSES)]
         diff = [
             [keep.tile([P, PACK, HALF], F32, name="diff%d%d" % (k, h)) for h in range(HALVES)]
             for k in range(PASSES)
         ]
-        share = [
-            [keep.tile([P, PACK, HALF], BF16, name="share%d%d" % (k, h)) for h in range(HALVES)]
-            for k in range(PASSES)
-        ]
-        dz_grouped = [
-            keep.tile([P, H, PACK], BF16, name="dz_grouped%d" % k, align_bytes=64)
-            for k in range(PASSES)
-        ]
-        x_grouped = [
-            keep.tile([P, F, PACK], BF16, name="x_grouped%d" % k, align_bytes=64)
-            for k in range(PASSES)
-        ]
+        share = {
+            (k, h): keep.tile([P, PACK, HALF], BF16, name="share%d%d" % (k, h)) for k, h in ((0, 0), (0, 1), (1, 0))
+        }
+        share_grouped = keep.tile([P, HALF, PACK], BF16, name="share_grouped")
+        dz_grouped = [keep.tile([P, H, PACK], BF16, name="dz_grouped%d" % k, align_bytes=64) for k in range(PASSES)]
+        x_grouped = [keep.tile([P, F, PACK], BF16, name="x_grouped%d" % k, align_bytes=64) for k in range(PASSES)]
         dz_codes = keep.tile([P, PASSES, H], U32, name="dz_codes", align_bytes=64)
         dz_scales = keep.tile([P, PASSES, H], U8, name="dz_scales", align_bytes=64)
         x_codes = keep.tile([P, PASSES, F], U32, name="x_codes", align_bytes=64)
         x_scales = keep.tile([P, PASSES, F], U8, name="x_scales", align_bytes=64)
-        acc = [psum.tile([M_TILE, H], F32, name="acc%d" % m) for m in range(M_TILES)]
         result = [keep.tile([M_TILE, H], F32, name="result%d" % m) for m in range(M_TILES)]
+        identity = keep.tile([P, P], BF16, name="identity")
+        make_identity(nc, identity[:])
 
-        pieces = [(0, 0), (0, 1), (1, 0), (1, 1)] + [(k, u) for u in range(2, UNITS) for k in range(PASSES)]
+        x_raw = {}
 
-        for k in range(PASSES):
-            for a in range(ROW_PAIRS):
-                pair = slice(2 * a, 2 * a + 2)
-                nc.sync.dma_start(out=c_raw[k][:, pair, :], in_=pass_rows(c, k)[:, pair, :])
-                nc.sync.dma_start(out=d_raw[k][:, pair, :], in_=pass_rows(d, k)[:, pair, :])
+        def load_cd(k):
+            nc.sync.dma_start(out=c_raw[k][:], in_=pass_rows(c, k))
+            for rows in (low, high):
+                nc.sync.dma_start(out=d_raw[k][:, rows, :], in_=pass_rows(d, k)[:, rows, :])
+
+        def load_g(k):
             nc.sync.dma_start(out=g_raw[k][:], in_=pass_rows(grad_out, k))
-            if k == 0:
-                nc.sync.dma_start(out=x_raw[0][:, :, 0 : 2 * UNIT], in_=pass_rows(x2, 0)[:, :, 0 : 2 * UNIT])
-        for k, u in pieces[2:]:
-            cols = slice(u * UNIT, (u + 1) * UNIT)
-            nc.sync.dma_start(out=x_raw[k][:, :, cols], in_=pass_rows(x2, k)[:, :, cols])
 
-        def compare(k, a, h):
-            pair = slice(2 * a, 2 * a + 2)
-            cols = slice(h * HALF, (h + 1) * HALF)
+        def load_x(k, first, count):
+            width = count * UNIT
+            tile = keep.tile([P, PACK, width], BF16, name="x_raw%d%d" % (k, first))
+            nc.sync.dma_start(out=tile[:], in_=pass_rows(x2, k)[:, :, first * UNIT : first * UNIT + width])
+            for n in range(count):
+                x_raw[(k, first + n)] = tile[:, :, n * UNIT : (n + 1) * UNIT]
+
+        load_cd(0)
+        load_g(0)
+        load_x(0, 0, 2)
+        load_cd(1)
+        load_g(1)
+        for k, first in ((1, 0), (0, 2), (1, 2)):
+            load_x(k, first, 2)
+
+        def subtract(k, h, rows):
             nc.vector.tensor_tensor(
-                out=diff[k][h][:, pair, :], in0=c_raw[k][:, pair, cols], in1=d_raw[k][:, pair, cols],
+                out=diff[k][h][:, rows, :], in0=c_raw[k][:, rows, half(h)], in1=d_raw[k][:, rows, half(h)],
                 op=ALU.subtract,
             )
-            nc.scalar.activation(out=share[k][h][:, pair, :], in_=diff[k][h][:, pair, :], func=ACT.Sigmoid, scale=STEEP)
+
+        def step(k, h, rows):
+            nc.scalar.activation(
+                out=share[(k, h)][:, rows, :], in_=diff[k][h][:, rows, :], func=ACT.Sigmoid, scale=STEEP
+            )
+
+        def step_grouped():
+            nc.scalar.activation(
+                out=share_grouped[:].rearrange("p (q i) j -> p q j i", i=4),
+                in_=diff[1][1][:].rearrange("p j (q i) -> p q j i", i=4),
+                func=ACT.Sigmoid,
+                scale=STEEP,
+            )
 
         def masked_gradient(k, h):
-            cols = slice(h * HALF, (h + 1) * HALF)
             nc.vector.tensor_tensor(
-                out=dz_grouped[k][:, cols, :].rearrange("p (q i) j -> p q j i", i=4),
-                in0=share[k][h][:].rearrange("p j (q i) -> p q j i", i=4),
-                in1=g_raw[k][:, :, cols].rearrange("p j (q i) -> p q j i", i=4),
+                out=dz_grouped[k][:, half(h), :].rearrange("p (q i) j -> p q j i", i=4),
+                in0=share[(k, h)][:].rearrange("p j (q i) -> p q j i", i=4),
+                in1=g_raw[k][:, :, half(h)].rearrange("p j (q i) -> p q j i", i=4),
                 op=ALU.mult,
             )
 
         def quantise_dz(k, h):
-            cols = slice(h * HALF, (h + 1) * HALF)
             nc.vector.quantize_mx(
-                out=dz_codes[:, k, cols].bitcast(E5M2_X4),
-                scales=dz_scales[:, k, cols],
-                in_=dz_grouped[k][:, cols, :].rearrange("p w j -> p (w j)"),
+                out=dz_codes[:, k, half(h)].bitcast(E5M2_X4),
+                scales=dz_scales[:, k, half(h)],
+                in_=dz_grouped[k][:, half(h), :].rearrange("p w j -> p (w j)"),
             )
 
         def regroup_x(copy, k, u):
-            cols = slice(u * UNIT, (u + 1) * UNIT)
             copy(
-                out=x_grouped[k][:, cols, :].rearrange("p (q i) j -> p q j i", i=4),
-                in_=x_raw[k][:, :, cols].rearrange("p j (q i) -> p q j i", i=4),
+                out=x_grouped[k][:, unit(u), :].rearrange("p (q i) j -> p q j i", i=4),
+                in_=x_raw[(k, u)].rearrange("p j (q i) -> p q j i", i=4),
             )
 
         def quantise_x(k, u):
-            cols = slice(u * UNIT, (u + 1) * UNIT)
             nc.vector.quantize_mx(
-                out=x_codes[:, k, cols].bitcast(E4M3_X4),
-                scales=x_scales[:, k, cols],
-                in_=x_grouped[k][:, cols, :].rearrange("p w j -> p (w j)"),
+                out=x_codes[:, k, unit(u)].bitcast(E4M3_X4),
+                scales=x_scales[:, k, unit(u)],
+                in_=x_grouped[k][:, unit(u), :].rearrange("p w j -> p (w j)"),
             )
+
+        acc = {}
 
         def multiply(k, m):
             rows = slice(m * M_TILE, (m + 1) * M_TILE)
+            if k == 0:
+                acc[m] = psum.tile([M_TILE, H], F32, name="acc%d" % m, tag="bank%d" % m)
             nc.tensor.matmul_mx(
                 out=acc[m][:],
                 lhsT=x_codes[:, k, rows].bitcast(E4M3_X4),
@@ -138,41 +159,91 @@ def tile_splitnn_pa_v_kernel(
                 stop=(k == PASSES - 1),
             )
 
-        def warm_up(moving):
+        def empty(copy, m):
+            copy(out=result[m][:], in_=acc[m][:])
+            nc.sync.dma_start(out=out[m * M_TILE : (m + 1) * M_TILE, :], in_=result[m][:])
+
+        ctx.enter_context(tc.manual_schedule())
+
+        for rows in (low, high):
+            for h in range(HALVES):
+                subtract(0, h, rows)
+                step(0, h, rows)
+        for h in range(HALVES):
+            masked_gradient(0, h)
+
+        for h in range(HALVES):
+            quantise_dz(0, h)
+
+        for u in range(2):
+            regroup_x(nc.scalar.copy, 0, u)
+        for u in range(2):
+            quantise_x(0, u)
+        for h in range(HALVES):
+            subtract(1, h, low)
+        step(1, 0, low)
+        for h in range(HALVES):
+            subtract(1, h, high)
+        step(1, 0, high)
+        step_grouped()
+        for m in (0, 1):
+            multiply(0, m)
+        g_grouped = psum.tile([P, HALF, PACK], BF16, name="g_grouped", tag="bank%d" % (M_TILES - 1))
+        for pair in (low, high):
             nc.tensor.matmul(
-                out=acc[M_TILES - 1][:], lhsT=g_raw[0][:, 0, 0:M_TILE], rhs=moving, start=True, stop=True
+                out=g_grouped[:, :, pair].rearrange("p w j -> p j w"),
+                lhsT=identity[:],
+                rhs=g_raw[1][:, pair, half(1)],
+                start=True,
+                stop=True,
             )
+        masked_gradient(1, 0)
+        nc.vector.tensor_tensor(
+            out=dz_grouped[1][:, half(1), :], in0=share_grouped[:], in1=g_grouped[:], op=ALU.mult
+        )
+        for m in (2, 3):
+            multiply(0, m)
+        idle = psum.tile([M_TILE, H], F32, name="idle", tag="bank%d" % (M_TILES - 2))
+        for part in range(2):
+            cols = slice(part * (HALF // 2), (part + 1) * (HALF // 2))
+            nc.tensor.matmul(
+                out=idle[:],
+                lhsT=identity[:],
+                rhs=dz_grouped[1][:, cols, :].rearrange("p w j -> p (w j)"),
+                start=True,
+                stop=True,
+            )
+        for h in range(HALVES):
+            quantise_dz(1, h)
 
-        for k in range(PASSES):
-            for a in range(ROW_PAIRS):
-                for h in range(HALVES):
-                    compare(k, a, h)
-            if k == PASSES - 1:
-                for h in range(HALVES):
-                    warm_up(share[k][h][:, 2:4, :].rearrange("p j w -> p (j w)"))
-            for h in range(HALVES):
-                masked_gradient(k, h)
-                if k == PASSES - 1:
-                    for part in range(2):
-                        cols = slice(h * HALF + part * (HALF // 2), h * HALF + (part + 1) * (HALF // 2))
-                        warm_up(dz_grouped[k][:, cols, :].rearrange("p w j -> p (w j)"))
-            for h in range(HALVES):
-                quantise_dz(k, h)
-
-        for k, u in pieces[:SCALAR_PIECES]:
-            regroup_x(nc.scalar.copy, k, u)
-
-        for u in range(UNITS):
-            for k in range(PASSES):
-                if (k, u) in pieces[SCALAR_PIECES:]:
-                    regroup_x(nc.vector.tensor_copy, k, u)
-            for k in range(PASSES):
-                quantise_x(k, u)
-            for m in range(u * UNIT // M_TILE, (u + 1) * UNIT // M_TILE):
-                for k in range(PASSES):
-                    multiply(k, m)
-                if m < M_TILES - 1:
-                    nc.scalar.copy(out=result[m][:], in_=acc[m][:])
-                else:
-                    nc.vector.tensor_copy(out=result[m][:], in_=acc[m][:])
-                nc.sync.dma_start(out=out[m * M_TILE : (m + 1) * M_TILE, :], in_=result[m][:])
+        regroup_x(nc.scalar.copy, 1, 0)
+        regroup_x(nc.scalar.copy, 0, 2)
+        quantise_x(1, 0)
+        for m in (0, 1):
+            multiply(1, m)
+        for m in (0, 1):
+            empty(nc.scalar.copy, m)
+        regroup_x(nc.vector.tensor_copy, 1, 1)
+        quantise_x(0, 2)
+        quantise_x(1, 1)
+        for m in (2, 3):
+            multiply(1, m)
+        for m in (2, 3):
+            empty(nc.scalar.copy, m)
+        regroup_x(nc.vector.tensor_copy, 1, 2)
+        regroup_x(nc.vector.tensor_copy, 0, 3)
+        quantise_x(1, 2)
+        for m in (4, 5):
+            multiply(0, m)
+            multiply(1, m)
+        for m in (4, 5):
+            empty(nc.scalar.copy, m)
+        regroup_x(nc.vector.tensor_copy, 1, 3)
+        quantise_x(0, 3)
+        for m in (6, 7):
+            multiply(0, m)
+        quantise_x(1, 3)
+        for m in (6, 7):
+            multiply(1, m)
+        empty(nc.scalar.copy, 6)
+        empty(nc.vector.tensor_copy, 7)

@@ -186,7 +186,7 @@ def tile_splitnn_pa_v_kernel(
             subtract(1, h, high)
         step(1, 0, high)
         step_grouped()
-        for m in (0, 1):
+        for m in range(4):
             multiply(0, m)
         g_grouped = psum.tile([P, HALF, PACK], BF16, name="g_grouped", tag="bank%d" % (M_TILES - 1))
         for pair in (low, high):
@@ -201,10 +201,8 @@ def tile_splitnn_pa_v_kernel(
         nc.vector.tensor_tensor(
             out=dz_grouped[1][:, half(1), :], in0=share_grouped[:], in1=g_grouped[:], op=ALU.mult
         )
-        for m in (2, 3):
-            multiply(0, m)
         idle = psum.tile([M_TILE, H], F32, name="idle", tag="bank%d" % (M_TILES - 2))
-        for part in range(2):
+        for part in range(4):
             cols = slice(part * (HALF // 2), (part + 1) * (HALF // 2))
             nc.tensor.matmul(
                 out=idle[:],
@@ -213,25 +211,21 @@ def tile_splitnn_pa_v_kernel(
                 start=True,
                 stop=True,
             )
+
+        regroup_x(nc.vector.tensor_copy, 1, 0)
+        regroup_x(nc.scalar.copy, 1, 1)
+        regroup_x(nc.scalar.copy, 0, 2)
         for h in range(HALVES):
             quantise_dz(1, h)
-
-        regroup_x(nc.scalar.copy, 1, 0)
-        regroup_x(nc.scalar.copy, 0, 2)
-        quantise_x(1, 0)
-        for m in (0, 1):
+        for u in range(2):
+            quantise_x(1, u)
+        for m in range(4):
             multiply(1, m)
-        for m in (0, 1):
+        for m in range(4):
             empty(nc.scalar.copy, m)
-        regroup_x(nc.vector.tensor_copy, 1, 1)
-        quantise_x(0, 2)
-        quantise_x(1, 1)
-        for m in (2, 3):
-            multiply(1, m)
-        for m in (2, 3):
-            empty(nc.scalar.copy, m)
-        regroup_x(nc.vector.tensor_copy, 1, 2)
         regroup_x(nc.vector.tensor_copy, 0, 3)
+        regroup_x(nc.vector.tensor_copy, 1, 2)
+        quantise_x(0, 2)
         quantise_x(1, 2)
         for m in (4, 5):
             multiply(0, m)
@@ -240,10 +234,9 @@ def tile_splitnn_pa_v_kernel(
             empty(nc.scalar.copy, m)
         regroup_x(nc.vector.tensor_copy, 1, 3)
         quantise_x(0, 3)
-        for m in (6, 7):
-            multiply(0, m)
         quantise_x(1, 3)
         for m in (6, 7):
+            multiply(0, m)
             multiply(1, m)
         empty(nc.scalar.copy, 6)
         empty(nc.vector.tensor_copy, 7)

@@ -81,20 +81,17 @@ def tile_splitnn_pa_v_kernel(
         def load_g(k):
             nc.sync.dma_start(out=g_raw[k][:], in_=pass_rows(grad_out, k))
 
-        def load_x(k, first, count):
-            width = count * UNIT
-            tile = keep.tile([P, PACK, width], BF16, name="x_raw%d%d" % (k, first))
-            nc.sync.dma_start(out=tile[:], in_=pass_rows(x2, k)[:, :, first * UNIT : first * UNIT + width])
-            for n in range(count):
-                x_raw[(k, first + n)] = tile[:, :, n * UNIT : (n + 1) * UNIT]
+        def load_x(k, u):
+            x_raw[(k, u)] = keep.tile([P, PACK, UNIT], BF16, name="x_raw%d%d" % (k, u))
+            nc.sync.dma_start(out=x_raw[(k, u)][:], in_=pass_rows(x2, k)[:, :, unit(u)])
 
         load_cd(0)
         load_g(0)
-        load_x(0, 0, 2)
+        load_x(0, 0)
         load_cd(1)
         load_g(1)
-        for k, first in ((1, 0), (0, 2), (1, 2)):
-            load_x(k, first, 2)
+        for k, u in ((1, 0), (0, 1), (1, 1), (0, 2), (1, 2), (0, 3), (1, 3)):
+            load_x(k, u)
 
         def subtract(k, h, rows):
             nc.vector.tensor_tensor(
@@ -133,7 +130,7 @@ def tile_splitnn_pa_v_kernel(
         def regroup_x(copy, k, u):
             copy(
                 out=x_grouped[k][:, unit(u), :].rearrange("p (q i) j -> p q j i", i=4),
-                in_=x_raw[(k, u)].rearrange("p j (q i) -> p q j i", i=4),
+                in_=x_raw[(k, u)][:].rearrange("p j (q i) -> p q j i", i=4),
             )
 
         def quantise_x(k, u):
@@ -142,6 +139,21 @@ def tile_splitnn_pa_v_kernel(
                 scales=x_scales[:, k, unit(u)],
                 in_=x_grouped[k][:, unit(u), :].rearrange("p w j -> p (w j)"),
             )
+
+        def by_identity(rows, bank):
+            grouped = psum.tile([P, UNIT, PACK], BF16, name="grouped%d" % bank, tag="bank%d" % bank)
+            for pair in (low, high):
+                nc.tensor.matmul(
+                    out=grouped[:, :, pair].rearrange("p w j -> p j w"),
+                    lhsT=identity[:],
+                    rhs=rows[:, pair, :],
+                    start=True,
+                    stop=True,
+                )
+            return grouped
+
+        def regroup_by_identity(k, u, bank):
+            nc.scalar.copy(out=x_grouped[k][:, unit(u), :], in_=by_identity(x_raw[(k, u)], bank)[:])
 
         acc = {}
 
@@ -175,10 +187,8 @@ def tile_splitnn_pa_v_kernel(
         for h in range(HALVES):
             quantise_dz(0, h)
 
-        for u in range(2):
-            regroup_x(nc.scalar.copy, 0, u)
-        for u in range(2):
-            quantise_x(0, u)
+        regroup_x(nc.scalar.copy, 0, 0)
+        quantise_x(0, 0)
         for h in range(HALVES):
             subtract(1, h, low)
         step(1, 0, low)
@@ -186,45 +196,34 @@ def tile_splitnn_pa_v_kernel(
             subtract(1, h, high)
         step(1, 0, high)
         step_grouped()
-        for m in range(4):
+        for m in (0, 1):
             multiply(0, m)
-        g_grouped = psum.tile([P, HALF, PACK], BF16, name="g_grouped", tag="bank%d" % (M_TILES - 1))
-        for pair in (low, high):
-            nc.tensor.matmul(
-                out=g_grouped[:, :, pair].rearrange("p w j -> p j w"),
-                lhsT=identity[:],
-                rhs=g_raw[1][:, pair, half(1)],
-                start=True,
-                stop=True,
-            )
+        g_grouped = by_identity(g_raw[1][:, :, half(1)], M_TILES - 1)
         masked_gradient(1, 0)
         nc.vector.tensor_tensor(
             out=dz_grouped[1][:, half(1), :], in0=share_grouped[:], in1=g_grouped[:], op=ALU.mult
         )
-        idle = psum.tile([M_TILE, H], F32, name="idle", tag="bank%d" % (M_TILES - 2))
-        for part in range(4):
-            cols = slice(part * (HALF // 2), (part + 1) * (HALF // 2))
-            nc.tensor.matmul(
-                out=idle[:],
-                lhsT=identity[:],
-                rhs=dz_grouped[1][:, cols, :].rearrange("p w j -> p (w j)"),
-                start=True,
-                stop=True,
-            )
-
-        regroup_x(nc.vector.tensor_copy, 1, 0)
-        regroup_x(nc.scalar.copy, 1, 1)
-        regroup_x(nc.scalar.copy, 0, 2)
         for h in range(HALVES):
             quantise_dz(1, h)
-        for u in range(2):
-            quantise_x(1, u)
-        for m in range(4):
+
+        regroup_x(nc.scalar.copy, 1, 0)
+        regroup_by_identity(0, 1, M_TILES - 2)
+        quantise_x(1, 0)
+        for m in (0, 1):
             multiply(1, m)
-        for m in range(4):
+        for m in (0, 1):
             empty(nc.scalar.copy, m)
-        regroup_x(nc.vector.tensor_copy, 0, 3)
+        regroup_by_identity(0, 2, M_TILES - 3)
+        regroup_x(nc.vector.tensor_copy, 1, 1)
+        quantise_x(0, 1)
+        quantise_x(1, 1)
+        for m in (2, 3):
+            multiply(0, m)
+            multiply(1, m)
+        for m in (2, 3):
+            empty(nc.scalar.copy, m)
         regroup_x(nc.vector.tensor_copy, 1, 2)
+        regroup_x(nc.vector.tensor_copy, 0, 3)
         quantise_x(0, 2)
         quantise_x(1, 2)
         for m in (4, 5):

from contextlib import ExitStack

import concourse.mybir as mybir
from concourse.masks import make_identity

F32 = mybir.dt.float32
BF16 = mybir.dt.bfloat16
U32 = mybir.dt.uint32
U8 = mybir.dt.uint8
E4M3_X4 = mybir.dt.float8_e4m3fn_x4
E5M2_X4 = mybir.dt.float8_e5m2_x4
ALU = mybir.AluOpType
ACT = mybir.ActivationFunctionType

B, F, H = 1024, 1024, 512
P = 128
PACK = 4
K_PASS = P * PACK
PASSES = B // K_PASS
HALVES = 2
HALF = H // HALVES
UNIT = 256
UNITS = F // UNIT
M_TILE = 128
M_TILES = F // M_TILE
STEEP = 2.0**100

FLOPS = 2 * B * F * H
BYTES = 2 * B * F + 2 * 4 * B * H + 2 * B * H + 4 * F * H


def tile_splitnn_pa_v_kernel(
    tc, x1, x2, W1, b1, W2, b2, noise_std, rr_uniform, c, d, grad_out, out
):
    nc = tc.nc

    def pass_rows(dram, k_pass):
        rows = dram[k_pass * K_PASS : (k_pass + 1) * K_PASS, :]
        return rows.rearrange("(p j) w -> p j w", j=PACK)

    def half(h):
        return slice(h * HALF, (h + 1) * HALF)

    def unit(u):
        return slice(u * UNIT, (u + 1) * UNIT)

    low, high = slice(0, 2), slice(2, 4)

    with ExitStack() as ctx:
        keep = ctx.enter_context(tc.tile_pool(name="keep", bufs=1))
        psum = ctx.enter_context(tc.psum_pool(name="psum", bufs=1))

        c_raw = [keep.tile([P, PACK, H], F32, name="c_raw%d" % k) for k in range(PASSES)]
        d_raw = [keep.tile([P, PACK, H], F32, name="d_raw%d" % k) for k in range(PASSES)]
        g_raw = [keep.tile([P, PACK, H], BF16, name="g_raw%d" % k) for k in range(PASSES)]
        diff = [
            [keep.tile([P, PACK, HALF], F32, name="diff%d%d" % (k, h)) for h in range(HALVES)]
            for k in range(PASSES)
        ]
        share = {
            (k, h): keep.tile([P, PACK, HALF], BF16, name="share%d%d" % (k, h)) for k, h in ((0, 0), (0, 1), (1, 0))
        }
        share_grouped = keep.tile([P, HALF, PACK], BF16, name="share_grouped")
        dz_grouped = [keep.tile([P, H, PACK], BF16, name="dz_grouped%d" % k, align_bytes=64) for k in range(PASSES)]
        x_grouped = [keep.tile([P, F, PACK], BF16, name="x_grouped%d" % k, align_bytes=64) for k in range(PASSES)]
        dz_codes = keep.tile([P, PASSES, H], U32, name="dz_codes", align_bytes=64)
        dz_scales = keep.tile([P, PASSES, H], U8, name="dz_scales", align_bytes=64)
        x_codes = keep.tile([P, PASSES, F], U32, name="x_codes", align_bytes=64)
        x_scales = keep.tile([P, PASSES, F], U8, name="x_scales", align_bytes=64)
        result = [keep.tile([M_TILE, H], F32, name="result%d" % m) for m in range(M_TILES)]
        identity = keep.tile([P, P], BF16, name="identity")
        make_identity(nc, identity[:])

        x_raw = {}

        def load_cd(k):
            nc.sync.dma_start(out=c_raw[k][:], in_=pass_rows(c, k))
            for rows in (low, high):
                nc.sync.dma_start(out=d_raw[k][:, rows, :], in_=pass_rows(d, k)[:, rows, :])

        def load_g(k):
            nc.sync.dma_start(out=g_raw[k][:], in_=pass_rows(grad_out, k))

        def load_x(k, u):
            x_raw[(k, u)] = keep.tile([P, PACK, UNIT], BF16, name="x_raw%d%d" % (k, u))
            nc.sync.dma_start(out=x_raw[(k, u)][:], in_=pass_rows(x2, k)[:, :, unit(u)])

        load_cd(0)
        load_g(0)
        load_x(0, 0)
        load_cd(1)
        load_g(1)
        for k, u in ((1, 0), (0, 1), (1, 1), (0, 2), (1, 2), (0, 3), (1, 3)):
            load_x(k, u)

        def subtract(k, h, rows):
            nc.vector.tensor_tensor(
                out=diff[k][h][:, rows, :], in0=c_raw[k][:, rows, half(h)], in1=d_raw[k][:, rows, half(h)],
                op=ALU.subtract,
            )

        def step(k, h, rows):
            nc.scalar.activation(
                out=share[(k, h)][:, rows, :], in_=diff[k][h][:, rows, :], func=ACT.Sigmoid, scale=STEEP
            )

        def step_grouped():
            nc.scalar.activation(
                out=share_grouped[:].rearrange("p (q i) j -> p q j i", i=4),
                in_=diff[1][1][:].rearrange("p j (q i) -> p q j i", i=4),
                func=ACT.Sigmoid,
                scale=STEEP,
            )

        def masked_gradient(k, h):
            nc.vector.tensor_tensor(
                out=dz_grouped[k][:, half(h), :].rearrange("p (q i) j -> p q j i", i=4),
                in0=share[(k, h)][:].rearrange("p j (q i) -> p q j i", i=4),
                in1=g_raw[k][:, :, half(h)].rearrange("p j (q i) -> p q j i", i=4),
                op=ALU.mult,
            )

        def quantise_dz(k, h):
            nc.vector.quantize_mx(
                out=dz_codes[:, k, half(h)].bitcast(E5M2_X4),
                scales=dz_scales[:, k, half(h)],
                in_=dz_grouped[k][:, half(h), :].rearrange("p w j -> p (w j)"),
            )

        def regroup_x(copy, k, u):
            copy(
                out=x_grouped[k][:, unit(u), :].rearrange("p (q i) j -> p q j i", i=4),
                in_=x_raw[(k, u)][:].rearrange("p j (q i) -> p q j i", i=4),
            )

        def quantise_x(k, u):
            nc.vector.quantize_mx(
                out=x_codes[:, k, unit(u)].bitcast(E4M3_X4),
                scales=x_scales[:, k, unit(u)],
                in_=x_grouped[k][:, unit(u), :].rearrange("p w j -> p (w j)"),
            )

        def by_identity(rows, bank):
            grouped = psum.tile([P, UNIT, PACK], BF16, name="grouped%d" % bank, tag="bank%d" % bank)
            for pair in (low, high):
                nc.tensor.matmul(
                    out=grouped[:, :, pair].rearrange("p w j -> p j w"),
                    lhsT=identity[:],
                    rhs=rows[:, pair, :],
                    start=True,
                    stop=True,
                )
            return grouped

        def regroup_by_identity(k, u, bank):
            nc.scalar.copy(out=x_grouped[k][:, unit(u), :], in_=by_identity(x_raw[(k, u)], bank)[:])

        acc = {}

        def multiply(k, m):
            rows = slice(m * M_TILE, (m + 1) * M_TILE)
            if k == 0:
                acc[m] = psum.tile([M_TILE, H], F32, name="acc%d" % m, tag="bank%d" % m)
            nc.tensor.matmul_mx(
                out=acc[m][:],
                lhsT=x_codes[:, k, rows].bitcast(E4M3_X4),
                lhsT_scale=x_scales[:, k, rows],
                rhs=dz_codes[:, k, :].bitcast(E5M2_X4),
                rhs_scale=dz_scales[:, k, :],
                start=(k == 0),
                stop=(k == PASSES - 1),
            )

        def empty(copy, m):
            copy(out=result[m][:], in_=acc[m][:])
            nc.sync.dma_start(out=out[m * M_TILE : (m + 1) * M_TILE, :], in_=result[m][:])

        ctx.enter_context(tc.manual_schedule())

        for rows in (low, high):
            for h in range(HALVES):
                subtract(0, h, rows)
                step(0, h, rows)
        for h in range(HALVES):
            masked_gradient(0, h)

        for h in range(HALVES):
            quantise_dz(0, h)

        regroup_x(nc.scalar.copy, 0, 0)
        quantise_x(0, 0)
        for h in range(HALVES):
            subtract(1, h, low)
        step(1, 0, low)
        for h in range(HALVES):
            subtract(1, h, high)
        step(1, 0, high)
        step_grouped()
        for m in (0, 1):
            multiply(0, m)
        g_grouped = by_identity(g_raw[1][:, :, half(1)], M_TILES - 1)
        masked_gradient(1, 0)
        nc.vector.tensor_tensor(
            out=dz_grouped[1][:, half(1), :], in0=share_grouped[:], in1=g_grouped[:], op=ALU.mult
        )
        for h in range(HALVES):
            quantise_dz(1, h)

        regroup_x(nc.scalar.copy, 1, 0)
        regroup_by_identity(0, 1, M_TILES - 2)
        quantise_x(1, 0)
        for m in (0, 1):
            multiply(1, m)
        for m in (0, 1):
            empty(nc.scalar.copy, m)
        regroup_by_identity(0, 2, M_TILES - 3)
        regroup_x(nc.vector.tensor_copy, 1, 1)
        quantise_x(0, 1)
        quantise_x(1, 1)
        for m in (2, 3):
            multiply(0, m)
            multiply(1, m)
        for m in (2, 3):
            empty(nc.scalar.copy, m)
        regroup_x(nc.vector.tensor_copy, 1, 2)
        regroup_x(nc.vector.tensor_copy, 0, 3)
        quantise_x(0, 2)
        quantise_x(1, 2)
        for m in (4, 5):
            multiply(0, m)
            multiply(1, m)
        for m in (4, 5):
            empty(nc.scalar.copy, m)
        regroup_x(nc.vector.tensor_copy, 1, 3)
        quantise_x(0, 3)
        quantise_x(1, 3)
        for m in (6, 7):
            multiply(0, m)
            multiply(1, m)
        empty(nc.scalar.copy, 6)
        empty(nc.vector.tensor_copy, 7)
